import numpy as np
import ml_dtypes


def mxq(x, axis, fmt="e4m3"):
    dtype, down = {"e4m3": (ml_dtypes.float8_e4m3fn, 7), "e5m2": (ml_dtypes.float8_e5m2, 14)}[fmt]
    v = np.moveaxis(np.asarray(x, np.float32).astype(ml_dtypes.bfloat16).astype(np.float64), axis, -1)
    blocks = v.reshape(v.shape[:-1] + (-1, 32))
    amax = np.abs(blocks).max(-1, keepdims=True)
    byte = np.maximum(np.where(amax > 0, np.frexp(amax)[1] - 1 + 127, 0) - down, 1)
    scale = np.exp2(byte - 127.0)
    codes = (blocks / scale).astype(np.float32).astype(dtype).astype(np.float64)
    return np.moveaxis((codes * scale).reshape(v.shape), -1, axis)


WIDE = False


def mx_kscale(k):
    if not WIDE:
        return np.ones(k)
    levels = np.array([10, -10, 5, -5, 0])
    a = np.random.permutation(np.resize(levels, k // 512 * 4)).reshape(k // 512, 4)
    idx = np.arange(k)
    return np.exp2(a[idx // 512, idx % 128 // 32])


BF16 = ml_dtypes.bfloat16


def bf(x):
    return np.asarray(x, np.float32).astype(BF16)


def f64(x):
    return np.asarray(x).astype(np.float64)


B, A, S, F = 128, 4, 128, 512


def setup_inputs():
    s, u = mx_kscale(F), mx_kscale(F)
    t, v = mx_kscale(F), mx_kscale(F)
    return {
        "h1": bf(np.maximum(np.random.standard_normal((B, A, F)) * 1.4, 0.0) * s),
        "W2": bf(np.random.standard_normal((A, F, F)) * 1.4 / np.sqrt(F) / s[:, None] * t),
        "b2": bf(np.random.standard_normal((A, F)) * 0.2 * t),
        "W3": bf(np.random.standard_normal((A, F, S)) / np.sqrt(F) / t[:, None]),
        "b3": bf(np.random.standard_normal((A, S)) * 0.2),
        "g1": bf(np.maximum(np.random.standard_normal((B, F)) * 1.4, 0.0) * u),
        "V2": bf(np.random.standard_normal((F, F)) * 1.4 / np.sqrt(F) / u[:, None] * v),
        "c2": bf(np.random.standard_normal(F) * 0.2 * v),
        "V3": bf(np.random.standard_normal((F, S)) / np.sqrt(F) / v[:, None]),
        "c3": bf(np.random.standard_normal(S) * 0.2),
    }


def reference(h1, W2, b2, W3, b3, g1, V2, c2, V3, c3):
    ha = mxq(f64(h1), 2, "e4m3").transpose(1, 0, 2)
    h2 = np.maximum((ha @ mxq(f64(W2), 1, "e4m3")) + f64(b2)[:, None, :], 0.0)
    psi_adv = ((mxq(h2, 2, "e4m3") @ mxq(f64(W3), 1, "e4m3")) + f64(b3)[:, None, :]).transpose(1, 0, 2)
    g2 = np.maximum((mxq(f64(g1), 1, "e4m3") @ mxq(f64(V2), 0, "e4m3")) + f64(c2), 0.0)
    psi_state = (mxq(g2, 1, "e4m3") @ mxq(f64(V3), 0, "e4m3")) + f64(c3)
    return psi_state[:, None, :] + psi_adv - psi_adv.mean(axis=1, keepdims=True)

@@ -1,0 +1,225 @@
+from contextlib import ExitStack
+
+import concourse.mybir as mybir
+from concourse.masks import make_identity
+
+F32 = mybir.dt.float32
+BF16 = mybir.dt.bfloat16
+U32 = mybir.dt.uint32
+U8 = mybir.dt.uint8
+FP8X4 = mybir.dt.float8_e4m3fn_x4
+ADD = mybir.AluOpType.add
+MULT = mybir.AluOpType.mult
+RELU = mybir.ActivationFunctionType.Relu
+
+P = 128
+PACK = 4
+B = 128
+A = 4
+F = 512
+S = 128
+NETS = A + 1
+STATE = A
+ORDER = [STATE, 0, 1, 2, 3]
+
+FLOPS = 2 * NETS * B * F * (F + S)
+
+
+def tile_psicritic_pa_s_kernel(tc, h1, W2, b2, W3, b3, g1, V2, c2, V3, c3, out):
+    nc = tc.nc
+    with ExitStack() as ctx:
+        keep = ctx.enter_context(tc.tile_pool(name="keep", bufs=1))
+        psum_two = ctx.enter_context(tc.psum_pool(name="psum_two", bufs=2))
+        psum_one = ctx.enter_context(tc.psum_pool(name="psum_one", bufs=1))
+
+        x_rows = keep.tile([P, NETS, F], BF16)
+        x_grouped = keep.tile([P, NETS, B, PACK], BF16, align_bytes=64)
+        x_codes = keep.tile([P, NETS, B], U32, align_bytes=64)
+        x_scales = keep.tile([P, NETS, B], U8, align_bytes=64)
+
+        wh_rows = keep.tile([P, NETS, PACK, F], BF16)
+        wh_grouped = keep.tile([P, NETS, PACK, P, PACK], BF16, align_bytes=64)
+        wh_codes = keep.tile([P, NETS, PACK, P], U32, align_bytes=64)
+        wh_scales = keep.tile([P, NETS, PACK, P], U8, align_bytes=64)
+
+        bh_bf16 = keep.tile([P, NETS, PACK], BF16)
+        bh = keep.tile([P, NETS, PACK], F32)
+
+        hid = keep.tile([P, NETS, PACK, B], BF16)
+        hid_grouped = keep.tile([P, NETS, B, PACK], BF16, align_bytes=64)
+        hid_codes = keep.tile([P, NETS, B], U32, align_bytes=64)
+        hid_scales = keep.tile([P, NETS, B], U8, align_bytes=64)
+
+        wo_rows = keep.tile([P, NETS, PACK, S], BF16)
+        wo_grouped = keep.tile([P, NETS, S, PACK], BF16, align_bytes=64)
+        wo_codes = keep.tile([P, NETS, S], U32, align_bytes=64)
+        wo_scales = keep.tile([P, NETS, S], U8, align_bytes=64)
+
+        identity = keep.tile([P, P], F32)
+        bias_rows = keep.tile([P, A, S], BF16)
+        bias_weight = keep.tile([P, P], BF16)
+        base = keep.tile([P, A, S], F32)
+        result = keep.tile([P, A, S], F32)
+
+        def load_hidden_weights(n, w):
+            nc.sync.dma_start(
+                out=wh_rows[:, n].rearrange("q (u e) f -> q u (e f)", u=2),
+                in_=w.rearrange("(u q e) f -> q u (e f)", u=2, e=2),
+            )
+
+        nc.sync.dma_start(out=x_rows[:, STATE, :], in_=g1)
+        load_hidden_weights(STATE, V2)
+        nc.sync.dma_start(out=x_rows[:, 0:A, :], in_=h1)
+        load_hidden_weights(0, W2[0])
+        nc.sync.dma_start(
+            out=wo_rows[:, STATE].rearrange("m j s -> m (j s)"),
+            in_=V3.rearrange("(m j) s -> m (j s)", j=PACK),
+        )
+        nc.sync.dma_start(
+            out=wo_rows[:, 0:A].rearrange("m a j s -> m a (j s)"),
+            in_=W3.rearrange("a (m j) s -> m a (j s)", j=PACK),
+        )
+        for a in range(1, A):
+            load_hidden_weights(a, W2[a])
+
+        nc.scalar.dma_start(out=bh_bf16[:, 0:A, :], in_=b2.rearrange("a (m j) -> m a j", j=PACK))
+        nc.scalar.dma_start(out=bh_bf16[:, STATE, :], in_=c2.rearrange("(m j) -> m j", j=PACK))
+        nc.vector.tensor_copy(out=bh[:], in_=bh_bf16[:])
+
+        make_identity(nc, identity[:])
+        nc.gpsimd.memset(bias_rows[:], 0.0)
+        nc.gpsimd.dma_start(out=bias_rows[0:1, :, :], in_=b3.rearrange("(o a) s -> o a s", o=1))
+        nc.gpsimd.dma_start(
+            out=bias_rows[1:2, :, :],
+            in_=c3.rearrange("(o r s) -> o r s", o=1, r=1).to_broadcast([1, A, S]),
+        )
+        nc.gpsimd.dma_start(out=bias_rows[32:36, :, :], in_=b3.unsqueeze(1).to_broadcast([A, A, S]))
+        nc.vector.memset(bias_weight[:], 1.0)
+        nc.vector.memset(bias_weight[32:64, :], -1.0 / A)
+
+        def transpose_x(n):
+            words = x_rows[:, n, :].bitcast(F32)
+            xt = psum_two.tile([P, 2, B], F32, tag="xt")
+            for u in range(2):
+                nc.tensor.transpose(xt[:, u, :], words[:, u * P : (u + 1) * P], identity[:])
+            nc.scalar.copy(
+                out=x_grouped[:, n].rearrange("q r t -> q (r t)").bitcast(F32).rearrange("q (r u) -> q r u", u=2),
+                in_=xt[:].rearrange("q u r -> q r u"),
+            )
+
+        def regroup_hidden_weights(n):
+            by_unit = wh_rows[:, n].rearrange("q t (m j) -> q j m t", j=PACK)
+            nc.vector.tensor_copy(out=wh_grouped[:, n, 0:2], in_=by_unit[:, 0:2])
+            nc.scalar.copy(out=wh_grouped[:, n, 2:4], in_=by_unit[:, 2:4])
+
+        def quantise_hidden_weights(n):
+            nc.vector.quantize_mx(
+                out=wh_codes[:, n].rearrange("q j m -> q (j m)").bitcast(FP8X4),
+                scales=wh_scales[:, n].rearrange("q j m -> q (j m)"),
+                in_=wh_grouped[:, n].rearrange("q j m t -> q (j m t)"),
+            )
+
+        def hidden_layer(n):
+            acc = psum_two.tile([P, PACK, B], F32, tag="acc")
+            for j in range(PACK):
+                nc.tensor.matmul_mx(
+                    out=acc[:, j, :],
+                    lhsT=wh_codes[:, n, j, :].bitcast(FP8X4),
+                    lhsT_scale=wh_scales[:, n, j, :],
+                    rhs=x_codes[:, n, :].bitcast(FP8X4),
+                    rhs_scale=x_scales[:, n, :],
+                    start=True,
+                    stop=True,
+                )
+            for j in range(PACK):
+                nc.scalar.activation(out=hid[:, n, j, :], in_=acc[:, j, :], func=RELU, bias=bh[:, n, j : j + 1])
+            nc.vector.tensor_copy(
+                out=hid_grouped[:, n].rearrange("m (c i) j -> m c j i", i=4),
+                in_=hid[:, n].rearrange("m j (c i) -> m c j i", i=4),
+            )
+            nc.vector.quantize_mx(
+                out=hid_codes[:, n, :].bitcast(FP8X4),
+                scales=hid_scales[:, n, :],
+                in_=hid_grouped[:, n].rearrange("m r j -> m (r j)"),
+            )
+
+        def head_pass(n, target, start, stop):
+            nc.tensor.matmul_mx(
+                out=target,
+                lhsT=hid_codes[:, n, :].bitcast(FP8X4),
+                lhsT_scale=hid_scales[:, n, :],
+                rhs=wo_codes[:, n, :].bitcast(FP8X4),
+                rhs_scale=wo_scales[:, n, :],
+                start=start,
+                stop=stop,
+            )
+
+        def head_layer(n):
+            head = psum_two.tile([P, S], F32, tag="head")
+            head_pass(n, head[:], True, True)
+            if n == STATE:
+                nc.vector.tensor_tensor(
+                    out=base[:], in0=base[:], in1=head[:].unsqueeze(1).to_broadcast([P, A, S]), op=ADD
+                )
+            else:
+                head_pass(n, adv_sum[:], n == 0, n == A - 1)
+                nc.vector.tensor_tensor(out=base[:, n, :], in0=base[:, n, :], in1=head[:], op=ADD)
+
+        transpose_x(STATE)
+        nc.vector.quantize_mx(
+            out=x_codes[:, STATE, :].bitcast(FP8X4),
+            scales=x_scales[:, STATE, :],
+            in_=x_grouped[:, STATE].rearrange("q r t -> q (r t)"),
+        )
+        regroup_hidden_weights(STATE)
+        quantise_hidden_weights(STATE)
+
+        for a in range(A):
+            transpose_x(a)
+        nc.vector.quantize_mx(
+            out=x_codes[:, 0:A, :].rearrange("q a r -> q (a r)").bitcast(FP8X4),
+            scales=x_scales[:, 0:A, :].rearrange("q a r -> q (a r)"),
+            in_=x_grouped[:, 0:A].rearrange("q a r t -> q (a r t)"),
+        )
+
+        beta = psum_one.tile([P, A, S], F32)
+        nc.tensor.matmul(
+            beta[:].rearrange("r a s -> r (a s)"),
+            lhsT=bias_weight[:],
+            rhs=bias_rows[:].rearrange("k a s -> k (a s)"),
+            start=True,
+            stop=True,
+        )
+        nc.scalar.copy(out=base[:], in_=beta[:])
+
+        nc.vector.tensor_copy(out=wo_grouped[:, STATE], in_=wo_rows[:, STATE].rearrange("m j s -> m s j"))
+        nc.vector.tensor_copy(out=wo_grouped[:, 0:2], in_=wo_rows[:, 0:2].rearrange("m a j s -> m a s j"))
+        nc.scalar.copy(out=wo_grouped[:, 2:4], in_=wo_rows[:, 2:4].rearrange("m a j s -> m a s j"))
+        nc.vector.quantize_mx(
+            out=wo_codes[:, STATE, :].bitcast(FP8X4),
+            scales=wo_scales[:, STATE, :],
+            in_=wo_grouped[:, STATE].rearrange("m s j -> m (s j)"),
+        )
+        nc.vector.quantize_mx(
+            out=wo_codes[:, 0:A, :].rearrange("m a s -> m (a s)").bitcast(FP8X4),
+            scales=wo_scales[:, 0:A, :].rearrange("m a s -> m (a s)"),
+            in_=wo_grouped[:, 0:A].rearrange("m a s j -> m (a s j)"),
+        )
+
+        adv_sum = psum_one.tile([P, S], F32)
+        for i in range(NETS):
+            if i + 1 < NETS:
+                regroup_hidden_weights(ORDER[i + 1])
+                quantise_hidden_weights(ORDER[i + 1])
+            hidden_layer(ORDER[i])
+            head_layer(ORDER[i])
+
+        nc.vector.scalar_tensor_tensor(
+            out=result[:],
+            in0=adv_sum[:].unsqueeze(1).to_broadcast([P, A, S]),
+            scalar=-1.0 / A,
+            in1=base[:],
+            op0=MULT,
+            op1=ADD,
+        )
+        nc.sync.dma_start(out=out, in_=result[:])

@@ -21,6 +21,7 @@ S = 128
 NETS = A + 1
 STATE = A
 ORDER = [STATE, 0, 1, 2, 3]
+VECTOR_UNITS = 96
 
 FLOPS = 2 * NETS * B * F * (F + S)
 
@@ -61,20 +62,36 @@ def tile_psicritic_pa_s_kernel(tc, h1, W2, b2, W3, b3, g1, V2, c2, V3, c3, out):
         base = keep.tile([P, A, S], F32)
         result = keep.tile([P, A, S], F32)
 
+        ctx.enter_context(tc.manual_schedule())
+
+        nc.scalar.dma_start(out=bh_bf16[:, 0:A, :], in_=b2.rearrange("a (m j) -> m a j", j=PACK))
+        nc.scalar.dma_start(out=bh_bf16[:, STATE, :], in_=c2.rearrange("(m j) -> m j", j=PACK))
+
+        nc.vector.memset(bias_rows[:], 0.0)
+        nc.scalar.dma_start(out=bias_rows[0:1, :, :], in_=b3.rearrange("(o a) s -> o a s", o=1))
+        nc.scalar.dma_start(
+            out=bias_rows[1:2, :, :],
+            in_=c3.rearrange("(o r s) -> o r s", o=1, r=1).to_broadcast([1, A, S]),
+        )
+        nc.scalar.dma_start(out=bias_rows[32:36, :, :], in_=b3.unsqueeze(1).to_broadcast([A, A, S]))
+        nc.vector.memset(bias_weight[:], 1.0)
+        nc.vector.memset(bias_weight[32:64, :], -1.0 / A)
+        make_identity(nc, identity[:])
+
         def load_hidden_weights(n, w):
             nc.sync.dma_start(
                 out=wh_rows[:, n].rearrange("q (u e) f -> q u (e f)", u=2),
                 in_=w.rearrange("(u q e) f -> q u (e f)", u=2, e=2),
             )
 
-        nc.sync.dma_start(out=x_rows[:, STATE, :], in_=g1)
         load_hidden_weights(STATE, V2)
-        nc.sync.dma_start(out=x_rows[:, 0:A, :], in_=h1)
-        load_hidden_weights(0, W2[0])
+        nc.sync.dma_start(out=x_rows[:, STATE, :], in_=g1)
         nc.sync.dma_start(
             out=wo_rows[:, STATE].rearrange("m j s -> m (j s)"),
             in_=V3.rearrange("(m j) s -> m (j s)", j=PACK),
         )
+        nc.sync.dma_start(out=x_rows[:, 0:A, :], in_=h1)
+        load_hidden_weights(0, W2[0])
         nc.sync.dma_start(
             out=wo_rows[:, 0:A].rearrange("m a j s -> m a (j s)"),
             in_=W3.rearrange("a (m j) s -> m a (j s)", j=PACK),
@@ -82,35 +99,32 @@ def tile_psicritic_pa_s_kernel(tc, h1, W2, b2, W3, b3, g1, V2, c2, V3, c3, out):
         for a in range(1, A):
             load_hidden_weights(a, W2[a])
 
-        nc.scalar.dma_start(out=bh_bf16[:, 0:A, :], in_=b2.rearrange("a (m j) -> m a j", j=PACK))
-        nc.scalar.dma_start(out=bh_bf16[:, STATE, :], in_=c2.rearrange("(m j) -> m j", j=PACK))
-        nc.vector.tensor_copy(out=bh[:], in_=bh_bf16[:])
-
-        make_identity(nc, identity[:])
-        nc.gpsimd.memset(bias_rows[:], 0.0)
-        nc.gpsimd.dma_start(out=bias_rows[0:1, :, :], in_=b3.rearrange("(o a) s -> o a s", o=1))
-        nc.gpsimd.dma_start(
-            out=bias_rows[1:2, :, :],
-            in_=c3.rearrange("(o r s) -> o r s", o=1, r=1).to_broadcast([1, A, S]),
-        )
-        nc.gpsimd.dma_start(out=bias_rows[32:36, :, :], in_=b3.unsqueeze(1).to_broadcast([A, A, S]))
-        nc.vector.memset(bias_weight[:], 1.0)
-        nc.vector.memset(bias_weight[32:64, :], -1.0 / A)
-
-        def transpose_x(n):
-            words = x_rows[:, n, :].bitcast(F32)
-            xt = psum_two.tile([P, 2, B], F32, tag="xt")
-            for u in range(2):
-                nc.tensor.transpose(xt[:, u, :], words[:, u * P : (u + 1) * P], identity[:])
+        def transpose_x(first, count):
+            xt = psum_two.tile([P, count, 2, B], F32, tag="xt")
+            for i in range(count):
+                words = x_rows[:, first + i, :].bitcast(F32)
+                for u in range(2):
+                    nc.tensor.transpose(xt[:, i, u, :], words[:, u * P : (u + 1) * P], identity[:])
             nc.scalar.copy(
-                out=x_grouped[:, n].rearrange("q r t -> q (r t)").bitcast(F32).rearrange("q (r u) -> q r u", u=2),
-                in_=xt[:].rearrange("q u r -> q r u"),
+                out=x_grouped[:, first : first + count]
+                .rearrange("q n r t -> q (n r t)")
+                .bitcast(F32)
+                .rearrange("q (n r u) -> q n r u", n=count, u=2),
+                in_=xt[:].rearrange("q n u r -> q n r u"),
+            )
+
+        def quantise_x(first, count):
+            nets = slice(first, first + count)
+            nc.vector.quantize_mx(
+                out=x_codes[:, nets, :].rearrange("q n r -> q (n r)").bitcast(FP8X4),
+                scales=x_scales[:, nets, :].rearrange("q n r -> q (n r)"),
+                in_=x_grouped[:, nets].rearrange("q n r t -> q (n r t)"),
             )
 
         def regroup_hidden_weights(n):
             by_unit = wh_rows[:, n].rearrange("q t (m j) -> q j m t", j=PACK)
-            nc.vector.tensor_copy(out=wh_grouped[:, n, 0:2], in_=by_unit[:, 0:2])
-            nc.scalar.copy(out=wh_grouped[:, n, 2:4], in_=by_unit[:, 2:4])
+            nc.vector.tensor_copy(out=wh_grouped[:, n, :, 0:VECTOR_UNITS], in_=by_unit[:, :, 0:VECTOR_UNITS])
+            nc.scalar.copy(out=wh_grouped[:, n, :, VECTOR_UNITS:P], in_=by_unit[:, :, VECTOR_UNITS:P])
 
         def quantise_hidden_weights(n):
             nc.vector.quantize_mx(
@@ -119,7 +133,22 @@ def tile_psicritic_pa_s_kernel(tc, h1, W2, b2, W3, b3, g1, V2, c2, V3, c3, out):
                 in_=wh_grouped[:, n].rearrange("q j m t -> q (j m t)"),
             )
 
-        def hidden_layer(n):
+        def regroup_head_weights(n, copy):
+            copy(
+                out=wo_grouped[:, n].rearrange("m (c i) j -> m c j i", i=4),
+                in_=wo_rows[:, n].rearrange("m j (c i) -> m c j i", i=4),
+            )
+
+        def quantise_head_weights(n):
+            nc.vector.quantize_mx(
+                out=wo_codes[:, n, :].bitcast(FP8X4),
+                scales=wo_scales[:, n, :],
+                in_=wo_grouped[:, n].rearrange("m s j -> m (s j)"),
+            )
+
+        sums = {}
+
+        def hidden_passes(n):
             acc = psum_two.tile([P, PACK, B], F32, tag="acc")
             for j in range(PACK):
                 nc.tensor.matmul_mx(
@@ -131,12 +160,21 @@ def tile_psicritic_pa_s_kernel(tc, h1, W2, b2, W3, b3, g1, V2, c2, V3, c3, out):
                     start=True,
                     stop=True,
                 )
+            sums[n] = acc
+
+        def bias_and_relu(n):
             for j in range(PACK):
-                nc.scalar.activation(out=hid[:, n, j, :], in_=acc[:, j, :], func=RELU, bias=bh[:, n, j : j + 1])
+                nc.scalar.activation(
+                    out=hid[:, n, j, :], in_=sums[n][:, j, :], func=RELU, bias=bh[:, n, j : j + 1]
+                )
+
+        def regroup_hidden(n):
             nc.vector.tensor_copy(
                 out=hid_grouped[:, n].rearrange("m (c i) j -> m c j i", i=4),
                 in_=hid[:, n].rearrange("m j (c i) -> m c j i", i=4),
             )
+
+        def quantise_hidden(n):
             nc.vector.quantize_mx(
                 out=hid_codes[:, n, :].bitcast(FP8X4),
                 scales=hid_scales[:, n, :],
@@ -154,35 +192,24 @@ def tile_psicritic_pa_s_kernel(tc, h1, W2, b2, W3, b3, g1, V2, c2, V3, c3, out):
                 stop=stop,
             )
 
-        def head_layer(n):
+        heads = {}
+
+        def head_passes(a):
             head = psum_two.tile([P, S], F32, tag="head")
-            head_pass(n, head[:], True, True)
-            if n == STATE:
-                nc.vector.tensor_tensor(
-                    out=base[:], in0=base[:], in1=head[:].unsqueeze(1).to_broadcast([P, A, S]), op=ADD
-                )
-            else:
-                head_pass(n, adv_sum[:], n == 0, n == A - 1)
-                nc.vector.tensor_tensor(out=base[:, n, :], in0=base[:, n, :], in1=head[:], op=ADD)
+            head_pass(STATE, head[:], True, False)
+            head_pass(a, head[:], False, True)
+            head_pass(a, adv_sum[:], a == 0, a == A - 1)
+            heads[a] = head
 
-        transpose_x(STATE)
-        nc.vector.quantize_mx(
-            out=x_codes[:, STATE, :].bitcast(FP8X4),
-            scales=x_scales[:, STATE, :],
-            in_=x_grouped[:, STATE].rearrange("q r t -> q (r t)"),
-        )
-        regroup_hidden_weights(STATE)
-        quantise_hidden_weights(STATE)
-
-        for a in range(A):
-            transpose_x(a)
-        nc.vector.quantize_mx(
-            out=x_codes[:, 0:A, :].rearrange("q a r -> q (a r)").bitcast(FP8X4),
-            scales=x_scales[:, 0:A, :].rearrange("q a r -> q (a r)"),
-            in_=x_grouped[:, 0:A].rearrange("q a r t -> q (a r t)"),
-        )
+        def add_head(a):
+            nc.vector.tensor_tensor(out=base[:, a, :], in0=base[:, a, :], in1=heads[a][:], op=ADD)
 
         beta = psum_one.tile([P, A, S], F32)
+        adv_sum = psum_one.tile([P, S], F32)
+
+        regroup_hidden_weights(STATE)
+        transpose_x(STATE, 1)
+        quantise_x(STATE, 1)
         nc.tensor.matmul(
             beta[:].rearrange("r a s -> r (a s)"),
             lhsT=bias_weight[:],
@@ -190,29 +217,35 @@ def tile_psicritic_pa_s_kernel(tc, h1, W2, b2, W3, b3, g1, V2, c2, V3, c3, out):
             start=True,
             stop=True,
         )
-        nc.scalar.copy(out=base[:], in_=beta[:])
+        transpose_x(0, 2)
+        transpose_x(2, 2)
+        quantise_hidden_weights(STATE)
+        hidden_passes(STATE)
+        nc.vector.tensor_copy(out=base[:], in_=beta[:])
+        nc.vector.tensor_copy(out=bh[:], in_=bh_bf16[:])
+        regroup_head_weights(STATE, nc.vector.tensor_copy)
 
-        nc.vector.tensor_copy(out=wo_grouped[:, STATE], in_=wo_rows[:, STATE].rearrange("m j s -> m s j"))
-        nc.vector.tensor_copy(out=wo_grouped[:, 0:2], in_=wo_rows[:, 0:2].rearrange("m a j s -> m a s j"))
-        nc.scalar.copy(out=wo_grouped[:, 2:4], in_=wo_rows[:, 2:4].rearrange("m a j s -> m a s j"))
-        nc.vector.quantize_mx(
-            out=wo_codes[:, STATE, :].bitcast(FP8X4),
-            scales=wo_scales[:, STATE, :],
-            in_=wo_grouped[:, STATE].rearrange("m s j -> m (s j)"),
-        )
-        nc.vector.quantize_mx(
-            out=wo_codes[:, 0:A, :].rearrange("m a s -> m (a s)").bitcast(FP8X4),
-            scales=wo_scales[:, 0:A, :].rearrange("m a s -> m (a s)"),
-            in_=wo_grouped[:, 0:A].rearrange("m a s j -> m (a s j)"),
-        )
-
-        adv_sum = psum_one.tile([P, S], F32)
-        for i in range(NETS):
-            if i + 1 < NETS:
-                regroup_hidden_weights(ORDER[i + 1])
-                quantise_hidden_weights(ORDER[i + 1])
-            hidden_layer(ORDER[i])
-            head_layer(ORDER[i])
+        for p in range(1, NETS + 2):
+            if p < NETS:
+                regroup_hidden_weights(ORDER[p])
+            if p == 1:
+                quantise_x(0, A)
+            if p <= NETS:
+                quantise_head_weights(ORDER[p - 1])
+            if p >= 2:
+                quantise_hidden(ORDER[p - 2])
+            if p >= 3:
+                head_passes(ORDER[p - 2])
+            if p < NETS:
+                quantise_hidden_weights(ORDER[p])
+                hidden_passes(ORDER[p])
+            if p >= 3:
+                add_head(ORDER[p - 2])
+            if p <= NETS:
+                bias_and_relu(ORDER[p - 1])
+                regroup_hidden(ORDER[p - 1])
+            if p < NETS:
+                regroup_head_weights(ORDER[p], nc.scalar.copy)
 
         nc.vector.scalar_tensor_tensor(
             out=result[:],

@@ -22,6 +22,7 @@ NETS = A + 1
 STATE = A
 ORDER = [STATE, 0, 1, 2, 3]
 VECTOR_UNITS = 96
+BLOCK = 16
 
 FLOPS = 2 * NETS * B * F * (F + S)
 
@@ -30,7 +31,7 @@ def tile_psicritic_pa_s_kernel(tc, h1, W2, b2, W3, b3, g1, V2, c2, V3, c3, out):
     nc = tc.nc
     with ExitStack() as ctx:
         keep = ctx.enter_context(tc.tile_pool(name="keep", bufs=1))
-        psum_two = ctx.enter_context(tc.psum_pool(name="psum_two", bufs=2))
+        psum_three = ctx.enter_context(tc.psum_pool(name="psum_three", bufs=3))
         psum_one = ctx.enter_context(tc.psum_pool(name="psum_one", bufs=1))
 
         x_rows = keep.tile([P, NETS, F], BF16)
@@ -43,7 +44,7 @@ def tile_psicritic_pa_s_kernel(tc, h1, W2, b2, W3, b3, g1, V2, c2, V3, c3, out):
         wh_codes = keep.tile([P, NETS, PACK, P], U32, align_bytes=64)
         wh_scales = keep.tile([P, NETS, PACK, P], U8, align_bytes=64)
 
-        bh_bf16 = keep.tile([P, NETS, PACK], BF16)
+        bh_bf16 = keep.tile([P, NETS, BLOCK], BF16)
         bh = keep.tile([P, NETS, PACK], F32)
 
         hid = keep.tile([P, NETS, PACK, B], BF16)
@@ -64,8 +65,8 @@ def tile_psicritic_pa_s_kernel(tc, h1, W2, b2, W3, b3, g1, V2, c2, V3, c3, out):
 
         ctx.enter_context(tc.manual_schedule())
 
-        nc.scalar.dma_start(out=bh_bf16[:, 0:A, :], in_=b2.rearrange("a (m j) -> m a j", j=PACK))
-        nc.scalar.dma_start(out=bh_bf16[:, STATE, :], in_=c2.rearrange("(m j) -> m j", j=PACK))
+        nc.scalar.dma_start(out=bh_bf16[:, 0:A, 0:PACK], in_=b2.rearrange("a (m j) -> m a j", j=PACK))
+        nc.scalar.dma_start(out=bh_bf16[:, STATE, 0:PACK], in_=c2.rearrange("(m j) -> m j", j=PACK))
 
         nc.vector.memset(bias_rows[:], 0.0)
         nc.scalar.dma_start(out=bias_rows[0:1, :, :], in_=b3.rearrange("(o a) s -> o a s", o=1))
@@ -85,22 +86,23 @@ def tile_psicritic_pa_s_kernel(tc, h1, W2, b2, W3, b3, g1, V2, c2, V3, c3, out):
             )
 
         load_hidden_weights(STATE, V2)
+        load_hidden_weights(0, W2[0])
         nc.sync.dma_start(out=x_rows[:, STATE, :], in_=g1)
+        nc.sync.dma_start(out=x_rows[:, 0:A, :], in_=h1)
+        load_hidden_weights(1, W2[1])
+        load_hidden_weights(2, W2[2])
         nc.sync.dma_start(
             out=wo_rows[:, STATE].rearrange("m j s -> m (j s)"),
             in_=V3.rearrange("(m j) s -> m (j s)", j=PACK),
         )
-        nc.sync.dma_start(out=x_rows[:, 0:A, :], in_=h1)
-        load_hidden_weights(0, W2[0])
         nc.sync.dma_start(
             out=wo_rows[:, 0:A].rearrange("m a j s -> m a (j s)"),
             in_=W3.rearrange("a (m j) s -> m a (j s)", j=PACK),
         )
-        for a in range(1, A):
-            load_hidden_weights(a, W2[a])
+        load_hidden_weights(3, W2[3])
 
         def transpose_x(first, count):
-            xt = psum_two.tile([P, count, 2, B], F32, tag="xt")
+            xt = psum_three.tile([P, count, 2, B], F32, tag="small")
             for i in range(count):
                 words = x_rows[:, first + i, :].bitcast(F32)
                 for u in range(2):
@@ -122,9 +124,10 @@ def tile_psicritic_pa_s_kernel(tc, h1, W2, b2, W3, b3, g1, V2, c2, V3, c3, out):
             )
 
         def regroup_hidden_weights(n):
-            by_unit = wh_rows[:, n].rearrange("q t (m j) -> q j m t", j=PACK)
-            nc.vector.tensor_copy(out=wh_grouped[:, n, :, 0:VECTOR_UNITS], in_=by_unit[:, :, 0:VECTOR_UNITS])
-            nc.scalar.copy(out=wh_grouped[:, n, :, VECTOR_UNITS:P], in_=by_unit[:, :, VECTOR_UNITS:P])
+            source = wh_rows[:, n].rearrange("q t (m j) -> q m t j", j=PACK)
+            target = wh_grouped[:, n].rearrange("q j m t -> q m t j")
+            nc.vector.tensor_copy(out=target[:, 0:VECTOR_UNITS], in_=source[:, 0:VECTOR_UNITS])
+            nc.scalar.copy(out=target[:, VECTOR_UNITS:P], in_=source[:, VECTOR_UNITS:P])
 
         def quantise_hidden_weights(n):
             nc.vector.quantize_mx(
@@ -149,7 +152,7 @@ def tile_psicritic_pa_s_kernel(tc, h1, W2, b2, W3, b3, g1, V2, c2, V3, c3, out):
         sums = {}
 
         def hidden_passes(n):
-            acc = psum_two.tile([P, PACK, B], F32, tag="acc")
+            acc = psum_three.tile([P, PACK, B], F32, tag="acc")
             for j in range(PACK):
                 nc.tensor.matmul_mx(
                     out=acc[:, j, :],
@@ -195,7 +198,7 @@ def tile_psicritic_pa_s_kernel(tc, h1, W2, b2, W3, b3, g1, V2, c2, V3, c3, out):
         heads = {}
 
         def head_passes(a):
-            head = psum_two.tile([P, S], F32, tag="head")
+            head = psum_three.tile([P, S], F32, tag="small")
             head_pass(STATE, head[:], True, False)
             head_pass(a, head[:], False, True)
             head_pass(a, adv_sum[:], a == 0, a == A - 1)
@@ -207,45 +210,47 @@ def tile_psicritic_pa_s_kernel(tc, h1, W2, b2, W3, b3, g1, V2, c2, V3, c3, out):
         beta = psum_one.tile([P, A, S], F32)
         adv_sum = psum_one.tile([P, S], F32)
 
-        regroup_hidden_weights(STATE)
-        transpose_x(STATE, 1)
-        quantise_x(STATE, 1)
-        nc.tensor.matmul(
-            beta[:].rearrange("r a s -> r (a s)"),
-            lhsT=bias_weight[:],
-            rhs=bias_rows[:].rearrange("k a s -> k (a s)"),
-            start=True,
-            stop=True,
-        )
-        transpose_x(0, 2)
-        transpose_x(2, 2)
-        quantise_hidden_weights(STATE)
-        hidden_passes(STATE)
-        nc.vector.tensor_copy(out=base[:], in_=beta[:])
-        nc.vector.tensor_copy(out=bh[:], in_=bh_bf16[:])
-        regroup_head_weights(STATE, nc.vector.tensor_copy)
-
-        for p in range(1, NETS + 2):
-            if p < NETS:
-                regroup_hidden_weights(ORDER[p])
+        regroup_hidden_weights(ORDER[0])
+        for p in range(NETS):
+            if p + 1 < NETS:
+                regroup_hidden_weights(ORDER[p + 1])
+            if p == 0:
+                transpose_x(STATE, 1)
+                nc.tensor.matmul(
+                    beta[:].rearrange("r a s -> r (a s)"),
+                    lhsT=bias_weight[:],
+                    rhs=bias_rows[:].rearrange("k a s -> k (a s)"),
+                    start=True,
+                    stop=True,
+                )
+                transpose_x(0, 2)
+                transpose_x(2, 2)
+                quantise_x(STATE, 1)
             if p == 1:
                 quantise_x(0, A)
-            if p <= NETS:
-                quantise_head_weights(ORDER[p - 1])
+            quantise_hidden_weights(ORDER[p])
+            hidden_passes(ORDER[p])
+            if p == 0:
+                nc.vector.tensor_copy(out=base[:], in_=beta[:])
+                nc.vector.tensor_copy(out=bh[:], in_=bh_bf16[:, :, 0:PACK])
             if p >= 2:
-                quantise_hidden(ORDER[p - 2])
-            if p >= 3:
-                head_passes(ORDER[p - 2])
-            if p < NETS:
-                quantise_hidden_weights(ORDER[p])
-                hidden_passes(ORDER[p])
-            if p >= 3:
-                add_head(ORDER[p - 2])
-            if p <= NETS:
+                regroup_head_weights(ORDER[p - 2], nc.scalar.copy)
+            if p >= 1:
                 bias_and_relu(ORDER[p - 1])
-                regroup_hidden(ORDER[p - 1])
-            if p < NETS:
-                regroup_head_weights(ORDER[p], nc.scalar.copy)
+        bias_and_relu(ORDER[NETS - 1])
+
+        for i in range(NETS - 2, NETS):
+            regroup_head_weights(ORDER[i], nc.vector.tensor_copy)
+        for i in range(NETS):
+            regroup_hidden(ORDER[i])
+            quantise_head_weights(ORDER[i])
+            quantise_hidden(ORDER[i])
+            if i >= 1:
+                head_passes(ORDER[i])
+            if i >= 3:
+                add_head(ORDER[i - 2])
+        add_head(ORDER[NETS - 2])
+        add_head(ORDER[NETS - 1])
 
         nc.vector.scalar_tensor_tensor(
             out=result[:],

@@ -22,6 +22,7 @@ NETS = A + 1
 STATE = A
 ORDER = [STATE, 0, 1, 2, 3]
 VECTOR_UNITS = 96
+SCALAR_HEADS = 2
 BLOCK = 16
 
 FLOPS = 2 * NETS * B * F * (F + S)
@@ -88,9 +89,11 @@ def tile_psicritic_pa_s_kernel(tc, h1, W2, b2, W3, b3, g1, V2, c2, V3, c3, out):
         load_hidden_weights(STATE, V2)
         load_hidden_weights(0, W2[0])
         nc.sync.dma_start(out=x_rows[:, STATE, :], in_=g1)
-        nc.sync.dma_start(out=x_rows[:, 0:A, :], in_=h1)
+        nc.sync.dma_start(out=x_rows[:, 0:2, :], in_=h1[:, 0:2, :])
         load_hidden_weights(1, W2[1])
+        nc.sync.dma_start(out=x_rows[:, 2:4, :], in_=h1[:, 2:4, :])
         load_hidden_weights(2, W2[2])
+        load_hidden_weights(3, W2[3])
         nc.sync.dma_start(
             out=wo_rows[:, STATE].rearrange("m j s -> m (j s)"),
             in_=V3.rearrange("(m j) s -> m (j s)", j=PACK),
@@ -99,7 +102,6 @@ def tile_psicritic_pa_s_kernel(tc, h1, W2, b2, W3, b3, g1, V2, c2, V3, c3, out):
             out=wo_rows[:, 0:A].rearrange("m a j s -> m a (j s)"),
             in_=W3.rearrange("a (m j) s -> m a (j s)", j=PACK),
         )
-        load_hidden_weights(3, W2[3])
 
         def transpose_x(first, count):
             xt = psum_three.tile([P, count, 2, B], F32, tag="small")
@@ -123,11 +125,16 @@ def tile_psicritic_pa_s_kernel(tc, h1, W2, b2, W3, b3, g1, V2, c2, V3, c3, out):
                 in_=x_grouped[:, nets].rearrange("q n r t -> q (n r t)"),
             )
 
-        def regroup_hidden_weights(n):
+        def regroup_hidden_weights(n, copy, units):
             source = wh_rows[:, n].rearrange("q t (m j) -> q m t j", j=PACK)
             target = wh_grouped[:, n].rearrange("q j m t -> q m t j")
-            nc.vector.tensor_copy(out=target[:, 0:VECTOR_UNITS], in_=source[:, 0:VECTOR_UNITS])
-            nc.scalar.copy(out=target[:, VECTOR_UNITS:P], in_=source[:, VECTOR_UNITS:P])
+            copy(out=target[:, units], in_=source[:, units])
+
+        def vector_regroups(n):
+            regroup_hidden_weights(n, nc.vector.tensor_copy, slice(0, VECTOR_UNITS))
+
+        def scalar_regroups(n):
+            regroup_hidden_weights(n, nc.scalar.copy, slice(VECTOR_UNITS, P))
 
         def quantise_hidden_weights(n):
             nc.vector.quantize_mx(
@@ -210,10 +217,12 @@ def tile_psicritic_pa_s_kernel(tc, h1, W2, b2, W3, b3, g1, V2, c2, V3, c3, out):
         beta = psum_one.tile([P, A, S], F32)
         adv_sum = psum_one.tile([P, S], F32)
 
-        regroup_hidden_weights(ORDER[0])
+        vector_regroups(ORDER[0])
+        scalar_regroups(ORDER[0])
+        scalar_regroups(ORDER[1])
         for p in range(NETS):
             if p + 1 < NETS:
-                regroup_hidden_weights(ORDER[p + 1])
+                vector_regroups(ORDER[p + 1])
             if p == 0:
                 transpose_x(STATE, 1)
                 nc.tensor.matmul(
@@ -223,23 +232,28 @@ def tile_psicritic_pa_s_kernel(tc, h1, W2, b2, W3, b3, g1, V2, c2, V3, c3, out):
                     start=True,
                     stop=True,
                 )
+                nc.scalar.copy(out=base[:], in_=beta[:])
                 transpose_x(0, 2)
+            if p + 2 < NETS:
+                scalar_regroups(ORDER[p + 2])
+            if p == 0:
                 transpose_x(2, 2)
                 quantise_x(STATE, 1)
             if p == 1:
-                quantise_x(0, A)
+                quantise_x(0, 2)
+            if p == 2:
+                quantise_x(2, 2)
             quantise_hidden_weights(ORDER[p])
             hidden_passes(ORDER[p])
             if p == 0:
-                nc.vector.tensor_copy(out=base[:], in_=beta[:])
                 nc.vector.tensor_copy(out=bh[:], in_=bh_bf16[:, :, 0:PACK])
-            if p >= 2:
+            if 2 <= p < 2 + SCALAR_HEADS:
                 regroup_head_weights(ORDER[p - 2], nc.scalar.copy)
             if p >= 1:
                 bias_and_relu(ORDER[p - 1])
         bias_and_relu(ORDER[NETS - 1])
 
-        for i in range(NETS - 2, NETS):
+        for i in range(SCALAR_HEADS, NETS):
             regroup_head_weights(ORDER[i], nc.vector.tensor_copy)
         for i in range(NETS):
             regroup_hidden(ORDER[i])

@@ -21,9 +21,10 @@ S = 128
 NETS = A + 1
 STATE = A
 ORDER = [STATE, 0, 1, 2, 3]
-VECTOR_UNITS = 96
-SCALAR_HEADS = 2
 BLOCK = 16
+
+VECTOR_UNITS = 100
+SCALAR_HEADS = 2
 
 FLOPS = 2 * NETS * B * F * (F + S)
 
@@ -46,7 +47,6 @@ def tile_psicritic_pa_s_kernel(tc, h1, W2, b2, W3, b3, g1, V2, c2, V3, c3, out):
         wh_scales = keep.tile([P, NETS, PACK, P], U8, align_bytes=64)
 
         bh_bf16 = keep.tile([P, NETS, BLOCK], BF16)
-        bh = keep.tile([P, NETS, PACK], F32)
 
         hid = keep.tile([P, NETS, PACK, B], BF16)
         hid_grouped = keep.tile([P, NETS, B, PACK], BF16, align_bytes=64)
@@ -175,7 +175,7 @@ def tile_psicritic_pa_s_kernel(tc, h1, W2, b2, W3, b3, g1, V2, c2, V3, c3, out):
         def bias_and_relu(n):
             for j in range(PACK):
                 nc.scalar.activation(
-                    out=hid[:, n, j, :], in_=sums[n][:, j, :], func=RELU, bias=bh[:, n, j : j + 1]
+                    out=hid[:, n, j, :], in_=sums[n][:, j, :], func=RELU, bias=bh_bf16[:, n, j : j + 1]
                 )
 
         def regroup_hidden(n):
@@ -217,40 +217,39 @@ def tile_psicritic_pa_s_kernel(tc, h1, W2, b2, W3, b3, g1, V2, c2, V3, c3, out):
         beta = psum_one.tile([P, A, S], F32)
         adv_sum = psum_one.tile([P, S], F32)
 
+
         vector_regroups(ORDER[0])
         scalar_regroups(ORDER[0])
         scalar_regroups(ORDER[1])
-        for p in range(NETS):
+        vector_regroups(ORDER[1])
+        transpose_x(STATE, 1)
+        nc.tensor.matmul(
+            beta[:].rearrange("r a s -> r (a s)"),
+            lhsT=bias_weight[:],
+            rhs=bias_rows[:].rearrange("k a s -> k (a s)"),
+            start=True,
+            stop=True,
+        )
+        nc.scalar.copy(out=base[:], in_=beta[:])
+        transpose_x(0, 2)
+        scalar_regroups(ORDER[2])
+        transpose_x(2, 2)
+        quantise_x(STATE, 1)
+        quantise_hidden_weights(ORDER[0])
+        hidden_passes(ORDER[0])
+
+        for p in range(1, NETS):
             if p + 1 < NETS:
                 vector_regroups(ORDER[p + 1])
-            if p == 0:
-                transpose_x(STATE, 1)
-                nc.tensor.matmul(
-                    beta[:].rearrange("r a s -> r (a s)"),
-                    lhsT=bias_weight[:],
-                    rhs=bias_rows[:].rearrange("k a s -> k (a s)"),
-                    start=True,
-                    stop=True,
-                )
-                nc.scalar.copy(out=base[:], in_=beta[:])
-                transpose_x(0, 2)
             if p + 2 < NETS:
                 scalar_regroups(ORDER[p + 2])
-            if p == 0:
-                transpose_x(2, 2)
-                quantise_x(STATE, 1)
-            if p == 1:
-                quantise_x(0, 2)
-            if p == 2:
-                quantise_x(2, 2)
+            if p <= A // 2:
+                quantise_x(2 * (p - 1), 2)
             quantise_hidden_weights(ORDER[p])
             hidden_passes(ORDER[p])
-            if p == 0:
-                nc.vector.tensor_copy(out=bh[:], in_=bh_bf16[:, :, 0:PACK])
             if 2 <= p < 2 + SCALAR_HEADS:
                 regroup_head_weights(ORDER[p - 2], nc.scalar.copy)
-            if p >= 1:
-                bias_and_relu(ORDER[p - 1])
+            bias_and_relu(ORDER[p - 1])
         bias_and_relu(ORDER[NETS - 1])
 
         for i in range(SCALAR_HEADS, NETS):

from contextlib import ExitStack

import concourse.mybir as mybir
from concourse.masks import make_identity

F32 = mybir.dt.float32
BF16 = mybir.dt.bfloat16
U32 = mybir.dt.uint32
U8 = mybir.dt.uint8
FP8X4 = mybir.dt.float8_e4m3fn_x4
ADD = mybir.AluOpType.add
MULT = mybir.AluOpType.mult
RELU = mybir.ActivationFunctionType.Relu

P = 128
PACK = 4
B = 128
A = 4
F = 512
S = 128
NETS = A + 1
STATE = A
ORDER = [STATE, 0, 1, 2, 3]
BLOCK = 16

VECTOR_UNITS = 100
SCALAR_HEADS = 2

FLOPS = 2 * NETS * B * F * (F + S)


def tile_psicritic_pa_s_kernel(tc, h1, W2, b2, W3, b3, g1, V2, c2, V3, c3, out):
    nc = tc.nc
    with ExitStack() as ctx:
        keep = ctx.enter_context(tc.tile_pool(name="keep", bufs=1))
        psum_three = ctx.enter_context(tc.psum_pool(name="psum_three", bufs=3))
        psum_one = ctx.enter_context(tc.psum_pool(name="psum_one", bufs=1))

        x_rows = keep.tile([P, NETS, F], BF16)
        x_grouped = keep.tile([P, NETS, B, PACK], BF16, align_bytes=64)
        x_codes = keep.tile([P, NETS, B], U32, align_bytes=64)
        x_scales = keep.tile([P, NETS, B], U8, align_bytes=64)

        wh_rows = keep.tile([P, NETS, PACK, F], BF16)
        wh_grouped = keep.tile([P, NETS, PACK, P, PACK], BF16, align_bytes=64)
        wh_codes = keep.tile([P, NETS, PACK, P], U32, align_bytes=64)
        wh_scales = keep.tile([P, NETS, PACK, P], U8, align_bytes=64)

        bh_bf16 = keep.tile([P, NETS, BLOCK], BF16)

        hid = keep.tile([P, NETS, PACK, B], BF16)
        hid_grouped = keep.tile([P, NETS, B, PACK], BF16, align_bytes=64)
        hid_codes = keep.tile([P, NETS, B], U32, align_bytes=64)
        hid_scales = keep.tile([P, NETS, B], U8, align_bytes=64)

        wo_rows = keep.tile([P, NETS, PACK, S], BF16)
        wo_grouped = keep.tile([P, NETS, S, PACK], BF16, align_bytes=64)
        wo_codes = keep.tile([P, NETS, S], U32, align_bytes=64)
        wo_scales = keep.tile([P, NETS, S], U8, align_bytes=64)

        identity = keep.tile([P, P], F32)
        bias_rows = keep.tile([P, A, S], BF16)
        bias_weight = keep.tile([P, P], BF16)
        base = keep.tile([P, A, S], F32)
        result = keep.tile([P, A, S], F32)

        ctx.enter_context(tc.manual_schedule())

        nc.scalar.dma_start(out=bh_bf16[:, 0:A, 0:PACK], in_=b2.rearrange("a (m j) -> m a j", j=PACK))
        nc.scalar.dma_start(out=bh_bf16[:, STATE, 0:PACK], in_=c2.rearrange("(m j) -> m j", j=PACK))

        nc.vector.memset(bias_rows[:], 0.0)
        nc.scalar.dma_start(out=bias_rows[0:1, :, :], in_=b3.rearrange("(o a) s -> o a s", o=1))
        nc.scalar.dma_start(
            out=bias_rows[1:2, :, :],
            in_=c3.rearrange("(o r s) -> o r s", o=1, r=1).to_broadcast([1, A, S]),
        )
        nc.scalar.dma_start(out=bias_rows[32:36, :, :], in_=b3.unsqueeze(1).to_broadcast([A, A, S]))
        nc.vector.memset(bias_weight[:], 1.0)
        nc.vector.memset(bias_weight[32:64, :], -1.0 / A)
        make_identity(nc, identity[:])

        def load_hidden_weights(n, w):
            nc.sync.dma_start(
                out=wh_rows[:, n].rearrange("q (u e) f -> q u (e f)", u=2),
                in_=w.rearrange("(u q e) f -> q u (e f)", u=2, e=2),
            )

        load_hidden_weights(STATE, V2)
        load_hidden_weights(0, W2[0])
        nc.sync.dma_start(out=x_rows[:, STATE, :], in_=g1)
        nc.sync.dma_start(out=x_rows[:, 0:2, :], in_=h1[:, 0:2, :])
        load_hidden_weights(1, W2[1])
        nc.sync.dma_start(out=x_rows[:, 2:4, :], in_=h1[:, 2:4, :])
        load_hidden_weights(2, W2[2])
        load_hidden_weights(3, W2[3])
        nc.sync.dma_start(
            out=wo_rows[:, STATE].rearrange("m j s -> m (j s)"),
            in_=V3.rearrange("(m j) s -> m (j s)", j=PACK),
        )
        nc.sync.dma_start(
            out=wo_rows[:, 0:A].rearrange("m a j s -> m a (j s)"),
            in_=W3.rearrange("a (m j) s -> m a (j s)", j=PACK),
        )

        def transpose_x(first, count):
            xt = psum_three.tile([P, count, 2, B], F32, tag="small")
            for i in range(count):
                words = x_rows[:, first + i, :].bitcast(F32)
                for u in range(2):
                    nc.tensor.transpose(xt[:, i, u, :], words[:, u * P : (u + 1) * P], identity[:])
            nc.scalar.copy(
                out=x_grouped[:, first : first + count]
                .rearrange("q n r t -> q (n r t)")
                .bitcast(F32)
                .rearrange("q (n r u) -> q n r u", n=count, u=2),
                in_=xt[:].rearrange("q n u r -> q n r u"),
            )

        def quantise_x(first, count):
            nets = slice(first, first + count)
            nc.vector.quantize_mx(
                out=x_codes[:, nets, :].rearrange("q n r -> q (n r)").bitcast(FP8X4),
                scales=x_scales[:, nets, :].rearrange("q n r -> q (n r)"),
                in_=x_grouped[:, nets].rearrange("q n r t -> q (n r t)"),
            )

        def regroup_hidden_weights(n, copy, units):
            source = wh_rows[:, n].rearrange("q t (m j) -> q m t j", j=PACK)
            target = wh_grouped[:, n].rearrange("q j m t -> q m t j")
            copy(out=target[:, units], in_=source[:, units])

        def vector_regroups(n):
            regroup_hidden_weights(n, nc.vector.tensor_copy, slice(0, VECTOR_UNITS))

        def scalar_regroups(n):
            regroup_hidden_weights(n, nc.scalar.copy, slice(VECTOR_UNITS, P))

        def quantise_hidden_weights(n):
            nc.vector.quantize_mx(
                out=wh_codes[:, n].rearrange("q j m -> q (j m)").bitcast(FP8X4),
                scales=wh_scales[:, n].rearrange("q j m -> q (j m)"),
                in_=wh_grouped[:, n].rearrange("q j m t -> q (j m t)"),
            )

        def regroup_head_weights(n, copy):
            copy(
                out=wo_grouped[:, n].rearrange("m (c i) j -> m c j i", i=4),
                in_=wo_rows[:, n].rearrange("m j (c i) -> m c j i", i=4),
            )

        def quantise_head_weights(n):
            nc.vector.quantize_mx(
                out=wo_codes[:, n, :].bitcast(FP8X4),
                scales=wo_scales[:, n, :],
                in_=wo_grouped[:, n].rearrange("m s j -> m (s j)"),
            )

        sums = {}

        def hidden_passes(n):
            acc = psum_three.tile([P, PACK, B], F32, tag="acc")
            for j in range(PACK):
                nc.tensor.matmul_mx(
                    out=acc[:, j, :],
                    lhsT=wh_codes[:, n, j, :].bitcast(FP8X4),
                    lhsT_scale=wh_scales[:, n, j, :],
                    rhs=x_codes[:, n, :].bitcast(FP8X4),
                    rhs_scale=x_scales[:, n, :],
                    start=True,
                    stop=True,
                )
            sums[n] = acc

        def bias_and_relu(n):
            for j in range(PACK):
                nc.scalar.activation(
                    out=hid[:, n, j, :], in_=sums[n][:, j, :], func=RELU, bias=bh_bf16[:, n, j : j + 1]
                )

        def regroup_hidden(n):
            nc.vector.tensor_copy(
                out=hid_grouped[:, n].rearrange("m (c i) j -> m c j i", i=4),
                in_=hid[:, n].rearrange("m j (c i) -> m c j i", i=4),
            )

        def quantise_hidden(n):
            nc.vector.quantize_mx(
                out=hid_codes[:, n, :].bitcast(FP8X4),
                scales=hid_scales[:, n, :],
                in_=hid_grouped[:, n].rearrange("m r j -> m (r j)"),
            )

        def head_pass(n, target, start, stop):
            nc.tensor.matmul_mx(
                out=target,
                lhsT=hid_codes[:, n, :].bitcast(FP8X4),
                lhsT_scale=hid_scales[:, n, :],
                rhs=wo_codes[:, n, :].bitcast(FP8X4),
                rhs_scale=wo_scales[:, n, :],
                start=start,
                stop=stop,
            )

        heads = {}

        def head_passes(a):
            head = psum_three.tile([P, S], F32, tag="small")
            head_pass(STATE, head[:], True, False)
            head_pass(a, head[:], False, True)
            head_pass(a, adv_sum[:], a == 0, a == A - 1)
            heads[a] = head

        def add_head(a):
            nc.vector.tensor_tensor(out=base[:, a, :], in0=base[:, a, :], in1=heads[a][:], op=ADD)

        beta = psum_one.tile([P, A, S], F32)
        adv_sum = psum_one.tile([P, S], F32)


        vector_regroups(ORDER[0])
        scalar_regroups(ORDER[0])
        scalar_regroups(ORDER[1])
        vector_regroups(ORDER[1])
        transpose_x(STATE, 1)
        nc.tensor.matmul(
            beta[:].rearrange("r a s -> r (a s)"),
            lhsT=bias_weight[:],
            rhs=bias_rows[:].rearrange("k a s -> k (a s)"),
            start=True,
            stop=True,
        )
        nc.scalar.copy(out=base[:], in_=beta[:])
        transpose_x(0, 2)
        scalar_regroups(ORDER[2])
        transpose_x(2, 2)
        quantise_x(STATE, 1)
        quantise_hidden_weights(ORDER[0])
        hidden_passes(ORDER[0])

        for p in range(1, NETS):
            if p + 1 < NETS:
                vector_regroups(ORDER[p + 1])
            if p + 2 < NETS:
                scalar_regroups(ORDER[p + 2])
            if p <= A // 2:
                quantise_x(2 * (p - 1), 2)
            quantise_hidden_weights(ORDER[p])
            hidden_passes(ORDER[p])
            if 2 <= p < 2 + SCALAR_HEADS:
                regroup_head_weights(ORDER[p - 2], nc.scalar.copy)
            bias_and_relu(ORDER[p - 1])
        bias_and_relu(ORDER[NETS - 1])

        for i in range(SCALAR_HEADS, NETS):
            regroup_head_weights(ORDER[i], nc.vector.tensor_copy)
        for i in range(NETS):
            regroup_hidden(ORDER[i])
            quantise_head_weights(ORDER[i])
            quantise_hidden(ORDER[i])
            if i >= 1:
                head_passes(ORDER[i])
            if i >= 3:
                add_head(ORDER[i - 2])
        add_head(ORDER[NETS - 2])
        add_head(ORDER[NETS - 1])

        nc.vector.scalar_tensor_tensor(
            out=result[:],
            in0=adv_sum[:].unsqueeze(1).to_broadcast([P, A, S]),
            scalar=-1.0 / A,
            in1=base[:],
            op0=MULT,
            op1=ADD,
        )
        nc.sync.dma_start(out=out, in_=result[:])
